import numpy as np
import ml_dtypes


def mxq(x, axis, fmt="e4m3"):
    dtype, down = {"e4m3": (ml_dtypes.float8_e4m3fn, 7), "e5m2": (ml_dtypes.float8_e5m2, 14)}[fmt]
    v = np.moveaxis(np.asarray(x, np.float32).astype(ml_dtypes.bfloat16).astype(np.float64), axis, -1)
    blocks = v.reshape(v.shape[:-1] + (-1, 32))
    amax = np.abs(blocks).max(-1, keepdims=True)
    byte = np.maximum(np.where(amax > 0, np.frexp(amax)[1] - 1 + 127, 0) - down, 1)
    scale = np.exp2(byte - 127.0)
    codes = (blocks / scale).astype(np.float32).astype(dtype).astype(np.float64)
    return np.moveaxis((codes * scale).reshape(v.shape), -1, axis)


WIDE = False


def mx_kscale(k):
    if not WIDE:
        return np.ones(k)
    levels = np.array([10, -10, 5, -5, 0])
    if k % 512:
        return np.exp2(np.random.permutation(np.resize(levels, k // 32))).repeat(32)
    a = np.empty((k // 512, 16))
    for p in range(k // 512):
        a[p, :8] = np.random.permutation(np.resize(levels, 8))
        for g in range(8):
            far = levels[np.abs(levels - a[p, g]) >= 10]
            a[p, g + 8] = far[np.random.randint(len(far))]
    return np.exp2(a.ravel()).repeat(32)


BF16 = ml_dtypes.bfloat16


def bf(x):
    return np.asarray(x, np.float32).astype(BF16)


def f64(x):
    return np.asarray(x).astype(np.float64)


B, H, W, C, I, O, NH = 1, 2, 512, 512, 512, 512, 8
DH = I // NH
SCALE = DH ** -0.5


def setup_inputs():
    s, t = mx_kscale(C), mx_kscale(I)
    sc = s[None, :, None, None]
    return {"left_feat": bf(np.random.standard_normal((B, C, H, W)) * sc),
            "right_feat": bf(np.random.standard_normal((B, C, H, W)) * sc),
            "wq": bf(np.random.standard_normal((I, C)) / np.sqrt(C) / s[None, :] * t[:, None]),
            "wk": bf(np.random.standard_normal((I, C)) / np.sqrt(C) / s[None, :] / t[:, None])}


def reference(left_feat, right_feat, wq, wk):
    lf = f64(left_feat).reshape(B, C, H * W)
    rf = f64(right_feat).reshape(B, C, H * W)
    q = f64(bf(mxq(f64(wq), 1, "e4m3") @ mxq(lf, 1, "e4m3")))
    k = f64(bf(mxq(f64(wk), 1, "e4m3") @ mxq(rf, 1, "e4m3")))
    q = q.reshape(B, I, H, W).transpose(0, 2, 3, 1)
    k = k.reshape(B, I, H, W).transpose(0, 2, 1, 3)
    return (mxq(q, 3, "e4m3") @ mxq(k, 2, "e4m3")) * SCALE

@@ -1,0 +1,279 @@
+from contextlib import ExitStack
+
+import concourse.mybir as mybir
+from concourse.masks import make_identity
+
+F32 = mybir.dt.float32
+BF16 = mybir.dt.bfloat16
+U32 = mybir.dt.uint32
+U8 = mybir.dt.uint8
+FP8X4 = mybir.dt.float8_e4m3fn_x4
+STAGE1_PSUM = BF16
+
+P = 128
+PACK = 4
+CHANNELS = 512
+WIDTH = 512
+GROUP = 128
+UNIT = 2 * GROUP
+HALF = CHANNELS // 2
+PSUM_BANKS = 8
+SCALE = 0.125
+
+FLOPS = 2 * 2 * CHANNELS * CHANNELS * 2 * WIDTH + 2 * 2 * WIDTH * WIDTH * CHANNELS
+
+SIDES = ("l", "r")
+
+UNITS = (
+    ("l", 0, 0),
+    ("l", 0, 1),
+    ("r", 0, 0),
+    ("r", 0, 1),
+    ("r", 1, 0),
+    ("r", 1, 1),
+    ("l", 1, 0),
+    ("l", 1, 1),
+)
+
+LAG = 2
+assert LAG == len(SIDES)
+
+SCORE_STEPS = {
+    5: ((0, 0),),
+    6: ((0, 1), (0, 2)),
+    7: ((0, 3),),
+    8: ((1, 0), (1, 1)),
+    9: ((1, 2), (1, 3)),
+}
+
+VECTOR_EMPTIES_UNITS = (5, 7)
+VECTOR_EMPTIES_SCORES = ((1, 1), (1, 3))
+
+WARM_UP_AT_START = 4
+WARM_UP_BETWEEN_WEIGHTS = 2
+
+
+def tile_sttm_single_pa_kernel(tc, left_feat, right_feat, wq, wk, out):
+    nc = tc.nc
+    with ExitStack() as ctx:
+        keep = ctx.enter_context(tc.tile_pool(name="keep", bufs=1))
+        psum = ctx.enter_context(tc.psum_pool(name="psum", bufs=PSUM_BANKS))
+        ctx.enter_context(tc.manual_schedule())
+
+        features = {
+            "l": left_feat[0].rearrange("(p j) h w -> p j h w", j=PACK),
+            "r": right_feat[0].rearrange("(p j) h w -> p j h w", j=PACK),
+        }
+        weights = {
+            "l": wq.rearrange("(m t) c -> m t c", t=PACK),
+            "r": wk.rearrange("(m t) c -> m t c", t=PACK),
+        }
+
+        w_raw = {}
+        w_grouped = {}
+        w_codes = {}
+        w_scales = {}
+        for side in SIDES:
+            w_raw[side] = keep.tile([P, PACK, CHANNELS], BF16, name="w_raw_" + side)
+            w_grouped[side] = keep.tile([P, CHANNELS * PACK], BF16, name="w_grouped_" + side, align_bytes=64)
+            w_codes[side] = keep.tile([P, CHANNELS], U32, name="w_codes_" + side, align_bytes=64)
+            w_scales[side] = keep.tile([P, CHANNELS], U8, name="w_scales_" + side, align_bytes=64)
+
+        x_raw = {}
+        x_grouped = {}
+        x_codes = {}
+        x_scales = {}
+        for unit in UNITS:
+            tail = "_%s%d%d" % unit
+            x_raw[unit] = keep.tile([P, PACK, UNIT], BF16, name="x_raw" + tail)
+            x_grouped[unit] = keep.tile([P, UNIT * PACK], BF16, name="x_grouped" + tail, align_bytes=64)
+            x_codes[unit] = keep.tile([P, UNIT], U32, name="x_codes" + tail, align_bytes=64)
+            x_scales[unit] = keep.tile([P, UNIT], U8, name="x_scales" + tail, align_bytes=64)
+
+        y_grouped = {}
+        y_codes = {}
+        y_scales = {}
+        scores_sb = {}
+        for h in range(2):
+            for side in SIDES:
+                tail = "_%s%d" % (side, h)
+                y_grouped[side, h] = keep.tile([P, WIDTH * PACK], BF16, name="y_grouped" + tail, align_bytes=64)
+                y_codes[side, h] = keep.tile([P, WIDTH], U32, name="y_codes" + tail, align_bytes=64)
+                y_scales[side, h] = keep.tile([P, WIDTH], U8, name="y_scales" + tail, align_bytes=64)
+            for wt in range(WIDTH // P):
+                scores_sb[h, wt] = keep.tile([P, WIDTH], F32, name="scores_sb_%d%d" % (h, wt))
+
+        banks = {}
+
+        def load_weights(side, half):
+            slots = slice(2 * half, 2 * half + 2)
+            nc.sync.dma_start(out=w_raw[side][:, slots, :], in_=weights[side][:, slots, :])
+
+        def load_features(unit):
+            side, h, part = unit
+            nc.sync.dma_start(out=x_raw[unit][:], in_=features[side][:, :, h, UNIT * part : UNIT * (part + 1)])
+
+        def warm_up(count):
+            for i in range(count):
+                nc.tensor.matmul(out=warm_bank[:], lhsT=zeros[:, WIDTH:], rhs=zeros[:, :WIDTH], start=True, stop=True)
+
+        def copy(engine, dst, src):
+            if engine == "scalar":
+                nc.scalar.copy(out=dst, in_=src)
+            else:
+                nc.vector.tensor_copy(out=dst, in_=src)
+
+        def transpose_weights(side, half):
+            bank = psum.tile([P, 2, 2, P], F32, tag="bank", name="w_bank_%s%d" % (side, half))
+            banks["w", side, half] = bank
+            words = w_raw[side][:].bitcast(F32)
+            for s in range(2):
+                for u in range(2):
+                    nc.tensor.transpose(bank[:, s, u, :], words[:, 2 * half + s, u : CHANNELS // 2 : 2], identity[:])
+
+        def group_weights(side, half):
+            dst = w_grouped[side][:, HALF * PACK * half : HALF * PACK * (half + 1)].bitcast(F32)
+            copy(
+                "scalar",
+                dst.rearrange("p (s m u) -> p s m u", s=2, u=2),
+                banks["w", side, half][:].rearrange("p s u m -> p s m u"),
+            )
+
+        def quantize_weights(side, half):
+            cols = slice(HALF * half, HALF * (half + 1))
+            nc.vector.quantize_mx(
+                out=w_codes[side][:, cols].bitcast(FP8X4),
+                scales=w_scales[side][:, cols],
+                in_=w_grouped[side][:, HALF * PACK * half : HALF * PACK * (half + 1)],
+            )
+
+        def interleave_features(unit):
+            nc.vector.tensor_copy(
+                out=x_grouped[unit][:].rearrange("p (b i j) -> p b j i", i=4, j=PACK),
+                in_=x_raw[unit][:].rearrange("p j (b i) -> p b j i", i=4),
+            )
+
+        def quantize_features(unit):
+            nc.vector.quantize_mx(out=x_codes[unit][:].bitcast(FP8X4), scales=x_scales[unit][:], in_=x_grouped[unit][:])
+
+        def project(unit, g):
+            side = unit[0]
+            bank = psum.tile([P, PACK, GROUP], STAGE1_PSUM, tag="bank", name="y_bank_%s%d%d%d" % (unit + (g,)))
+            banks["y", unit, g] = bank
+            positions = slice(GROUP * g, GROUP * (g + 1))
+            for t in range(PACK):
+                channels = slice(P * t, P * (t + 1))
+                nc.tensor.matmul_mx(
+                    out=bank[:, t, :],
+                    lhsT=w_codes[side][:, channels].bitcast(FP8X4),
+                    lhsT_scale=w_scales[side][:, channels],
+                    rhs=x_codes[unit][:, positions].bitcast(FP8X4),
+                    rhs_scale=x_scales[unit][:, positions],
+                    start=True,
+                    stop=True,
+                )
+
+        def group_projection(engine, unit, g):
+            side, h, part = unit
+            first = (UNIT * part + GROUP * g) * PACK
+            copy(
+                engine,
+                y_grouped[side, h][:, first : first + GROUP * PACK].rearrange("p (n t) -> p n t", t=PACK),
+                banks["y", unit, g][:].rearrange("p t n -> p n t"),
+            )
+
+        def quantize_projection(unit):
+            side, h, part = unit
+            positions = slice(UNIT * part, UNIT * (part + 1))
+            nc.vector.quantize_mx(
+                out=y_codes[side, h][:, positions].bitcast(FP8X4),
+                scales=y_scales[side, h][:, positions],
+                in_=y_grouped[side, h][:, UNIT * PACK * part : UNIT * PACK * (part + 1)],
+            )
+
+        def multiply_scores(h, wt):
+            bank = psum.tile([P, WIDTH], F32, tag="bank", name="scores_bank_%d%d" % (h, wt))
+            banks["scores", h, wt] = bank
+            rows = slice(P * wt, P * (wt + 1))
+            nc.tensor.matmul_mx(
+                out=bank[:],
+                lhsT=y_codes["l", h][:, rows].bitcast(FP8X4),
+                lhsT_scale=y_scales["l", h][:, rows],
+                rhs=y_codes["r", h][:].bitcast(FP8X4),
+                rhs_scale=y_scales["r", h][:],
+                start=True,
+                stop=True,
+            )
+
+        def store_scores(engine, h, wt):
+            if engine == "scalar":
+                nc.scalar.mul(scores_sb[h, wt][:], banks["scores", h, wt][:], SCALE)
+            else:
+                nc.vector.tensor_scalar_mul(scores_sb[h, wt][:], banks["scores", h, wt][:], SCALE)
+            nc.sync.dma_start(out=out[0, h, P * wt : P * (wt + 1), :], in_=scores_sb[h, wt][:])
+
+        load_weights("l", 0)
+        load_weights("l", 1)
+        load_features(UNITS[0])
+        load_weights("r", 0)
+        load_weights("r", 1)
+        for unit in UNITS[1:]:
+            load_features(unit)
+
+        identity = keep.tile([P, P], F32, name="identity")
+        make_identity(nc, identity[:])
+        table_in = keep.tile([P, 8], F32, name="table_in")
+        table_out = keep.tile([P, 8], F32, name="table_out")
+        nc.vector.memset(table_in[:], 0.0)
+        nc.scalar.mul(table_out[:], table_in[:], SCALE)
+        zeros = keep.tile([P, WIDTH + P], BF16, name="zeros")
+        nc.vector.memset(zeros[:], 0.0)
+        warm_bank = psum.tile([P, WIDTH], F32, tag="bank", name="warm_bank")
+
+        warm_up(WARM_UP_AT_START)
+        transpose_weights("l", 0)
+        transpose_weights("l", 1)
+        warm_up(WARM_UP_BETWEEN_WEIGHTS)
+        group_weights("l", 0)
+        group_weights("l", 1)
+        transpose_weights("r", 0)
+        transpose_weights("r", 1)
+        group_weights("r", 0)
+        group_weights("r", 1)
+
+        vector_reads = []
+        for step in range(len(UNITS) + LAG):
+            if step < len(UNITS):
+                interleave_features(UNITS[step])
+            if step < len(SIDES):
+                quantize_weights(SIDES[step], 0)
+            else:
+                quantize_projection(UNITS[step - LAG])
+            for read, args in vector_reads:
+                read("vector", *args)
+            vector_reads = []
+            if step < len(UNITS):
+                quantize_features(UNITS[step])
+            if step < len(SIDES):
+                quantize_weights(SIDES[step], 1)
+
+            tiles = SCORE_STEPS.get(step, ())
+            for h, wt in tiles:
+                multiply_scores(h, wt)
+            if step < len(UNITS):
+                project(UNITS[step], 0)
+                project(UNITS[step], 1)
+
+            for h, wt in tiles:
+                if (h, wt) in VECTOR_EMPTIES_SCORES:
+                    vector_reads.append((store_scores, (h, wt)))
+                else:
+                    store_scores("scalar", h, wt)
+            if step < len(UNITS):
+                group_projection("scalar", UNITS[step], 0)
+                if step in VECTOR_EMPTIES_UNITS:
+                    vector_reads.append((group_projection, (UNITS[step], 1)))
+                else:
+                    group_projection("scalar", UNITS[step], 1)
+        for read, args in vector_reads:
+            read("vector", *args)

@@ -22,32 +22,24 @@ SCALE = 0.125
 
 FLOPS = 2 * 2 * CHANNELS * CHANNELS * 2 * WIDTH + 2 * 2 * WIDTH * WIDTH * CHANNELS
 
-SIDES = ("l", "r")
+SIDES = ("r", "l")
 
 UNITS = (
-    ("l", 0, 0),
-    ("l", 0, 1),
     ("r", 0, 0),
     ("r", 0, 1),
+    ("l", 0, 0),
+    ("l", 0, 1),
     ("r", 1, 0),
     ("r", 1, 1),
     ("l", 1, 0),
     ("l", 1, 1),
 )
 
-LAG = 2
-assert LAG == len(SIDES)
+LAG = 3
+assert LAG == 1 + len(SIDES)
 
-SCORE_STEPS = {
-    5: ((0, 0),),
-    6: ((0, 1), (0, 2)),
-    7: ((0, 3),),
-    8: ((1, 0), (1, 1)),
-    9: ((1, 2), (1, 3)),
-}
-
-VECTOR_EMPTIES_UNITS = (5, 7)
-VECTOR_EMPTIES_SCORES = ((1, 1), (1, 3))
+VECTOR_READS_SCORES_AFTER = 1
+VECTOR_READS_PROJECTION_AFTER = 2
 
 WARM_UP_AT_START = 4
 WARM_UP_BETWEEN_WEIGHTS = 2
@@ -139,13 +131,8 @@ def tile_sttm_single_pa_kernel(tc, left_feat, right_feat, wq, wk, out):
                 banks["w", side, half][:].rearrange("p s u m -> p s m u"),
             )
 
-        def quantize_weights(side, half):
-            cols = slice(HALF * half, HALF * (half + 1))
-            nc.vector.quantize_mx(
-                out=w_codes[side][:, cols].bitcast(FP8X4),
-                scales=w_scales[side][:, cols],
-                in_=w_grouped[side][:, HALF * PACK * half : HALF * PACK * (half + 1)],
-            )
+        def quantize_weights(side):
+            nc.vector.quantize_mx(out=w_codes[side][:].bitcast(FP8X4), scales=w_scales[side][:], in_=w_grouped[side][:])
 
         def interleave_features(unit):
             nc.vector.tensor_copy(
@@ -212,12 +199,13 @@ def tile_sttm_single_pa_kernel(tc, left_feat, right_feat, wq, wk, out):
                 nc.vector.tensor_scalar_mul(scores_sb[h, wt][:], banks["scores", h, wt][:], SCALE)
             nc.sync.dma_start(out=out[0, h, P * wt : P * (wt + 1), :], in_=scores_sb[h, wt][:])
 
-        load_weights("l", 0)
-        load_weights("l", 1)
         load_features(UNITS[0])
-        load_weights("r", 0)
-        load_weights("r", 1)
-        for unit in UNITS[1:]:
+        load_weights(SIDES[0], 0)
+        load_weights(SIDES[0], 1)
+        load_features(UNITS[1])
+        load_weights(SIDES[1], 0)
+        load_weights(SIDES[1], 1)
+        for unit in UNITS[2:]:
             load_features(unit)
 
         identity = keep.tile([P, P], F32, name="identity")
@@ -231,49 +219,52 @@ def tile_sttm_single_pa_kernel(tc, left_feat, right_feat, wq, wk, out):
         warm_bank = psum.tile([P, WIDTH], F32, tag="bank", name="warm_bank")
 
         warm_up(WARM_UP_AT_START)
-        transpose_weights("l", 0)
-        transpose_weights("l", 1)
+        transpose_weights(SIDES[0], 0)
+        transpose_weights(SIDES[0], 1)
         warm_up(WARM_UP_BETWEEN_WEIGHTS)
-        group_weights("l", 0)
-        group_weights("l", 1)
-        transpose_weights("r", 0)
-        transpose_weights("r", 1)
-        group_weights("r", 0)
-        group_weights("r", 1)
+        group_weights(SIDES[0], 0)
+        group_weights(SIDES[0], 1)
+        transpose_weights(SIDES[1], 0)
+        transpose_weights(SIDES[1], 1)
+        group_weights(SIDES[1], 0)
+        group_weights(SIDES[1], 1)
 
         vector_reads = []
-        for step in range(len(UNITS) + LAG):
+        waiting = []
+        for step in range(len(UNITS) + LAG + 1):
             if step < len(UNITS):
                 interleave_features(UNITS[step])
-            if step < len(SIDES):
-                quantize_weights(SIDES[step], 0)
-            else:
+            if 1 <= step <= len(SIDES):
+                quantize_weights(SIDES[step - 1])
+            if LAG <= step < len(UNITS) + LAG:
                 quantize_projection(UNITS[step - LAG])
-            for read, args in vector_reads:
-                read("vector", *args)
-            vector_reads = []
+            for due, read, args in vector_reads:
+                if due == step:
+                    read("vector", *args)
             if step < len(UNITS):
                 quantize_features(UNITS[step])
-            if step < len(SIDES):
-                quantize_weights(SIDES[step], 1)
 
-            tiles = SCORE_STEPS.get(step, ())
-            for h, wt in tiles:
-                multiply_scores(h, wt)
+            tiles = ()
+            if LAG <= step < len(UNITS) + LAG and UNITS[step - LAG][0] == "l":
+                h, part = UNITS[step - LAG][1:]
+                tiles = ((h, 2 * part), (h, 2 * part + 1))
+                multiply_scores(*tiles[0])
+                multiply_scores(*tiles[1])
             if step < len(UNITS):
-                project(UNITS[step], 0)
-                project(UNITS[step], 1)
+                waiting.append(UNITS[step])
+            ready = waiting if step >= 1 else []
+            for unit in ready:
+                project(unit, 0)
+                project(unit, 1)
 
-            for h, wt in tiles:
-                if (h, wt) in VECTOR_EMPTIES_SCORES:
-                    vector_reads.append((store_scores, (h, wt)))
+            if tiles:
+                store_scores("scalar", *tiles[0])
+                vector_reads.append((step + VECTOR_READS_SCORES_AFTER, store_scores, tiles[1]))
+            for unit in ready:
+                group_projection("scalar", unit, 0)
+                if unit == UNITS[-1]:
+                    vector_reads.append((step + VECTOR_READS_PROJECTION_AFTER, group_projection, (unit, 1)))
                 else:
-                    store_scores("scalar", h, wt)
-            if step < len(UNITS):
-                group_projection("scalar", UNITS[step], 0)
-                if step in VECTOR_EMPTIES_UNITS:
-                    vector_reads.append((group_projection, (UNITS[step], 1)))
-                else:
-                    group_projection("scalar", UNITS[step], 1)
-        for read, args in vector_reads:
-            read("vector", *args)
+                    group_projection("scalar", unit, 1)
+            if step >= 1:
+                waiting = []

@@ -238,11 +238,11 @@ def tile_sttm_single_pa_kernel(tc, left_feat, right_feat, wq, wk, out):
                 quantize_weights(SIDES[step - 1])
             if LAG <= step < len(UNITS) + LAG:
                 quantize_projection(UNITS[step - LAG])
+            if step < len(UNITS):
+                quantize_features(UNITS[step])
             for due, read, args in vector_reads:
                 if due == step:
                     read("vector", *args)
-            if step < len(UNITS):
-                quantize_features(UNITS[step])
 
             tiles = ()
             if LAG <= step < len(UNITS) + LAG and UNITS[step - LAG][0] == "l":

@@ -38,6 +38,8 @@ UNITS = (
 LAG = 3
 assert LAG == 1 + len(SIDES)
 
+PIECE_WIDTH = (WIDTH, WIDTH // 2)
+
 VECTOR_READS_SCORES_AFTER = 1
 VECTOR_READS_PROJECTION_AFTER = 2
 
@@ -93,7 +95,8 @@ def tile_sttm_single_pa_kernel(tc, left_feat, right_feat, wq, wk, out):
                 y_codes[side, h] = keep.tile([P, WIDTH], U32, name="y_codes" + tail, align_bytes=64)
                 y_scales[side, h] = keep.tile([P, WIDTH], U8, name="y_scales" + tail, align_bytes=64)
             for wt in range(WIDTH // P):
-                scores_sb[h, wt] = keep.tile([P, WIDTH], F32, name="scores_sb_%d%d" % (h, wt))
+                for piece in range(WIDTH // PIECE_WIDTH[h]):
+                    scores_sb[h, wt, piece] = keep.tile([P, PIECE_WIDTH[h]], F32, name="scores_sb_%d%d%d" % (h, wt, piece))
 
         banks = {}
 
@@ -178,26 +181,31 @@ def tile_sttm_single_pa_kernel(tc, left_feat, right_feat, wq, wk, out):
                 in_=y_grouped[side, h][:, UNIT * PACK * part : UNIT * PACK * (part + 1)],
             )
 
-        def multiply_scores(h, wt):
-            bank = psum.tile([P, WIDTH], F32, tag="bank", name="scores_bank_%d%d" % (h, wt))
-            banks["scores", h, wt] = bank
+        def multiply_scores(h, wt, piece):
+            width = PIECE_WIDTH[h]
+            bank = psum.tile([P, width], F32, tag="bank", name="scores_bank_%d%d%d" % (h, wt, piece))
+            banks["scores", h, wt, piece] = bank
             rows = slice(P * wt, P * (wt + 1))
+            columns = slice(width * piece, width * (piece + 1))
             nc.tensor.matmul_mx(
                 out=bank[:],
                 lhsT=y_codes["l", h][:, rows].bitcast(FP8X4),
                 lhsT_scale=y_scales["l", h][:, rows],
-                rhs=y_codes["r", h][:].bitcast(FP8X4),
-                rhs_scale=y_scales["r", h][:],
+                rhs=y_codes["r", h][:, columns].bitcast(FP8X4),
+                rhs_scale=y_scales["r", h][:, columns],
                 start=True,
                 stop=True,
             )
 
-        def store_scores(engine, h, wt):
+        def store_scores(engine, h, wt, piece):
+            width = PIECE_WIDTH[h]
             if engine == "scalar":
-                nc.scalar.mul(scores_sb[h, wt][:], banks["scores", h, wt][:], SCALE)
+                nc.scalar.mul(scores_sb[h, wt, piece][:], banks["scores", h, wt, piece][:], SCALE)
             else:
-                nc.vector.tensor_scalar_mul(scores_sb[h, wt][:], banks["scores", h, wt][:], SCALE)
-            nc.sync.dma_start(out=out[0, h, P * wt : P * (wt + 1), :], in_=scores_sb[h, wt][:])
+                nc.vector.tensor_scalar_mul(scores_sb[h, wt, piece][:], banks["scores", h, wt, piece][:], SCALE)
+            nc.sync.dma_start(
+                out=out[0, h, P * wt : P * (wt + 1), width * piece : width * (piece + 1)], in_=scores_sb[h, wt, piece][:]
+            )
 
         load_features(UNITS[0])
         load_weights(SIDES[0], 0)
@@ -244,12 +252,14 @@ def tile_sttm_single_pa_kernel(tc, left_feat, right_feat, wq, wk, out):
                 if due == step:
                     read("vector", *args)
 
-            tiles = ()
+            pieces = []
             if LAG <= step < len(UNITS) + LAG and UNITS[step - LAG][0] == "l":
                 h, part = UNITS[step - LAG][1:]
-                tiles = ((h, 2 * part), (h, 2 * part + 1))
-                multiply_scores(*tiles[0])
-                multiply_scores(*tiles[1])
+                for wt in (2 * part, 2 * part + 1):
+                    for piece in range(WIDTH // PIECE_WIDTH[h]):
+                        pieces.append((h, wt, piece))
+            for piece in pieces:
+                multiply_scores(*piece)
             if step < len(UNITS):
                 waiting.append(UNITS[step])
             ready = waiting if step >= 1 else []
@@ -257,9 +267,10 @@ def tile_sttm_single_pa_kernel(tc, left_feat, right_feat, wq, wk, out):
                 project(unit, 0)
                 project(unit, 1)
 
-            if tiles:
-                store_scores("scalar", *tiles[0])
-                vector_reads.append((step + VECTOR_READS_SCORES_AFTER, store_scores, tiles[1]))
+            for piece in pieces[:-1]:
+                store_scores("scalar", *piece)
+            for piece in pieces[-1:]:
+                vector_reads.append((step + VECTOR_READS_SCORES_AFTER, store_scores, piece))
             for unit in ready:
                 group_projection("scalar", unit, 0)
                 if unit == UNITS[-1]:

@@ -15,7 +15,6 @@ PACK = 4
 CHANNELS = 512
 WIDTH = 512
 GROUP = 128
-UNIT = 2 * GROUP
 HALF = CHANNELS // 2
 PSUM_BANKS = 8
 SCALE = 0.125
@@ -25,23 +24,24 @@ FLOPS = 2 * 2 * CHANNELS * CHANNELS * 2 * WIDTH + 2 * 2 * WIDTH * WIDTH * CHANNE
 SIDES = ("r", "l")
 
 UNITS = (
-    ("r", 0, 0),
-    ("r", 0, 1),
-    ("l", 0, 0),
-    ("l", 0, 1),
-    ("r", 1, 0),
-    ("r", 1, 1),
-    ("l", 1, 0),
-    ("l", 1, 1),
+    ("r", 0, 0, 256),
+    ("r", 0, 256, 256),
+    ("l", 0, 0, 256),
+    ("l", 0, 256, 256),
+    ("r", 1, 0, 256),
+    ("l", 1, 0, 256),
+    ("l", 1, 256, 256),
+    ("r", 1, 256, 256),
 )
 
 LAG = 3
-assert LAG == 1 + len(SIDES)
 
 PIECE_WIDTH = (WIDTH, WIDTH // 2)
 
+VECTOR_PIECES = 1
+
 VECTOR_READS_SCORES_AFTER = 1
-VECTOR_READS_PROJECTION_AFTER = 2
+VECTOR_READS_PROJECTION_AFTER = 1
 
 WARM_UP_AT_START = 4
 WARM_UP_BETWEEN_WEIGHTS = 2
@@ -78,11 +78,12 @@ def tile_sttm_single_pa_kernel(tc, left_feat, right_feat, wq, wk, out):
         x_codes = {}
         x_scales = {}
         for unit in UNITS:
-            tail = "_%s%d%d" % unit
-            x_raw[unit] = keep.tile([P, PACK, UNIT], BF16, name="x_raw" + tail)
-            x_grouped[unit] = keep.tile([P, UNIT * PACK], BF16, name="x_grouped" + tail, align_bytes=64)
-            x_codes[unit] = keep.tile([P, UNIT], U32, name="x_codes" + tail, align_bytes=64)
-            x_scales[unit] = keep.tile([P, UNIT], U8, name="x_scales" + tail, align_bytes=64)
+            tail = "_%s%d_%d_%d" % unit
+            count = unit[3]
+            x_raw[unit] = keep.tile([P, PACK, count], BF16, name="x_raw" + tail)
+            x_grouped[unit] = keep.tile([P, count * PACK], BF16, name="x_grouped" + tail, align_bytes=64)
+            x_codes[unit] = keep.tile([P, count], U32, name="x_codes" + tail, align_bytes=64)
+            x_scales[unit] = keep.tile([P, count], U8, name="x_scales" + tail, align_bytes=64)
 
         y_grouped = {}
         y_codes = {}
@@ -95,8 +96,8 @@ def tile_sttm_single_pa_kernel(tc, left_feat, right_feat, wq, wk, out):
                 y_codes[side, h] = keep.tile([P, WIDTH], U32, name="y_codes" + tail, align_bytes=64)
                 y_scales[side, h] = keep.tile([P, WIDTH], U8, name="y_scales" + tail, align_bytes=64)
             for wt in range(WIDTH // P):
-                for piece in range(WIDTH // PIECE_WIDTH[h]):
-                    scores_sb[h, wt, piece] = keep.tile([P, PIECE_WIDTH[h]], F32, name="scores_sb_%d%d%d" % (h, wt, piece))
+                for part in range(WIDTH // PIECE_WIDTH[h]):
+                    scores_sb[h, wt, part] = keep.tile([P, PIECE_WIDTH[h]], F32, name="scores_sb_%d%d%d" % (h, wt, part))
 
         banks = {}
 
@@ -105,8 +106,8 @@ def tile_sttm_single_pa_kernel(tc, left_feat, right_feat, wq, wk, out):
             nc.sync.dma_start(out=w_raw[side][:, slots, :], in_=weights[side][:, slots, :])
 
         def load_features(unit):
-            side, h, part = unit
-            nc.sync.dma_start(out=x_raw[unit][:], in_=features[side][:, :, h, UNIT * part : UNIT * (part + 1)])
+            side, h, first, count = unit
+            nc.sync.dma_start(out=x_raw[unit][:], in_=features[side][:, :, h, first : first + count])
 
         def warm_up(count):
             for i in range(count):
@@ -135,7 +136,13 @@ def tile_sttm_single_pa_kernel(tc, left_feat, right_feat, wq, wk, out):
             )
 
         def quantize_weights(side):
-            nc.vector.quantize_mx(out=w_codes[side][:].bitcast(FP8X4), scales=w_scales[side][:], in_=w_grouped[side][:])
+            for half in range(2):
+                cols = slice(HALF * half, HALF * (half + 1))
+                nc.vector.quantize_mx(
+                    out=w_codes[side][:, cols].bitcast(FP8X4),
+                    scales=w_scales[side][:, cols],
+                    in_=w_grouped[side][:, HALF * PACK * half : HALF * PACK * (half + 1)],
+                )
 
         def interleave_features(unit):
             nc.vector.tensor_copy(
@@ -148,7 +155,7 @@ def tile_sttm_single_pa_kernel(tc, left_feat, right_feat, wq, wk, out):
 
         def project(unit, g):
             side = unit[0]
-            bank = psum.tile([P, PACK, GROUP], STAGE1_PSUM, tag="bank", name="y_bank_%s%d%d%d" % (unit + (g,)))
+            bank = psum.tile([P, PACK, GROUP], STAGE1_PSUM, tag="bank", name="y_bank_%s%d_%d_%d_%d" % (unit + (g,)))
             banks["y", unit, g] = bank
             positions = slice(GROUP * g, GROUP * (g + 1))
             for t in range(PACK):
@@ -164,29 +171,29 @@ def tile_sttm_single_pa_kernel(tc, left_feat, right_feat, wq, wk, out):
                 )
 
         def group_projection(engine, unit, g):
-            side, h, part = unit
-            first = (UNIT * part + GROUP * g) * PACK
+            side, h, first, count = unit
+            start = (first + GROUP * g) * PACK
             copy(
                 engine,
-                y_grouped[side, h][:, first : first + GROUP * PACK].rearrange("p (n t) -> p n t", t=PACK),
+                y_grouped[side, h][:, start : start + GROUP * PACK].rearrange("p (n t) -> p n t", t=PACK),
                 banks["y", unit, g][:].rearrange("p t n -> p n t"),
             )
 
         def quantize_projection(unit):
-            side, h, part = unit
-            positions = slice(UNIT * part, UNIT * (part + 1))
+            side, h, first, count = unit
+            positions = slice(first, first + count)
             nc.vector.quantize_mx(
                 out=y_codes[side, h][:, positions].bitcast(FP8X4),
                 scales=y_scales[side, h][:, positions],
-                in_=y_grouped[side, h][:, UNIT * PACK * part : UNIT * PACK * (part + 1)],
+                in_=y_grouped[side, h][:, first * PACK : (first + count) * PACK],
             )
 
-        def multiply_scores(h, wt, piece):
+        def multiply_scores(h, wt, part):
             width = PIECE_WIDTH[h]
-            bank = psum.tile([P, width], F32, tag="bank", name="scores_bank_%d%d%d" % (h, wt, piece))
-            banks["scores", h, wt, piece] = bank
+            bank = psum.tile([P, width], F32, tag="bank", name="scores_bank_%d%d%d" % (h, wt, part))
+            banks["scores", h, wt, part] = bank
             rows = slice(P * wt, P * (wt + 1))
-            columns = slice(width * piece, width * (piece + 1))
+            columns = slice(width * part, width * (part + 1))
             nc.tensor.matmul_mx(
                 out=bank[:],
                 lhsT=y_codes["l", h][:, rows].bitcast(FP8X4),
@@ -197,14 +204,14 @@ def tile_sttm_single_pa_kernel(tc, left_feat, right_feat, wq, wk, out):
                 stop=True,
             )
 
-        def store_scores(engine, h, wt, piece):
+        def store_scores(engine, h, wt, part):
             width = PIECE_WIDTH[h]
             if engine == "scalar":
-                nc.scalar.mul(scores_sb[h, wt, piece][:], banks["scores", h, wt, piece][:], SCALE)
+                nc.scalar.mul(scores_sb[h, wt, part][:], banks["scores", h, wt, part][:], SCALE)
             else:
-                nc.vector.tensor_scalar_mul(scores_sb[h, wt, piece][:], banks["scores", h, wt, piece][:], SCALE)
+                nc.vector.tensor_scalar_mul(scores_sb[h, wt, part][:], banks["scores", h, wt, part][:], SCALE)
             nc.sync.dma_start(
-                out=out[0, h, P * wt : P * (wt + 1), width * piece : width * (piece + 1)], in_=scores_sb[h, wt, piece][:]
+                out=out[0, h, P * wt : P * (wt + 1), width * part : width * (part + 1)], in_=scores_sb[h, wt, part][:]
             )
 
         load_features(UNITS[0])
@@ -237,6 +244,14 @@ def tile_sttm_single_pa_kernel(tc, left_feat, right_feat, wq, wk, out):
         group_weights(SIDES[1], 0)
         group_weights(SIDES[1], 1)
 
+        quantised = []
+        multiplied = []
+
+        def covered(side, h, first, end):
+            return sum(u[3] for u in quantised if u[0] == side and u[1] == h and first <= u[2] and u[2] + u[3] <= end) + sum(
+                end - first for u in quantised if u[0] == side and u[1] == h and u[2] <= first and end <= u[2] + u[3] and u[3] > end - first
+            ) == end - first
+
         vector_reads = []
         waiting = []
         for step in range(len(UNITS) + LAG + 1):
@@ -253,29 +268,35 @@ def tile_sttm_single_pa_kernel(tc, left_feat, right_feat, wq, wk, out):
                     read("vector", *args)
 
             pieces = []
-            if LAG <= step < len(UNITS) + LAG and UNITS[step - LAG][0] == "l":
-                h, part = UNITS[step - LAG][1:]
-                for wt in (2 * part, 2 * part + 1):
-                    for piece in range(WIDTH // PIECE_WIDTH[h]):
-                        pieces.append((h, wt, piece))
-            for piece in pieces:
-                multiply_scores(*piece)
+            if LAG <= step < len(UNITS) + LAG:
+                quantised.append(UNITS[step - LAG])
+                for h in range(2):
+                    for wt in range(WIDTH // P):
+                        for part in range(WIDTH // PIECE_WIDTH[h]):
+                            item = (h, wt, part)
+                            q_there = covered("l", h, P * wt, P * (wt + 1))
+                            k_there = covered("r", h, PIECE_WIDTH[h] * part, PIECE_WIDTH[h] * (part + 1))
+                            if item not in multiplied and q_there and k_there:
+                                pieces.append(item)
+                                multiplied.append(item)
+            for item in pieces:
+                multiply_scores(*item)
             if step < len(UNITS):
                 waiting.append(UNITS[step])
             ready = waiting if step >= 1 else []
             for unit in ready:
-                project(unit, 0)
-                project(unit, 1)
+                for g in range(unit[3] // GROUP):
+                    project(unit, g)
 
-            for piece in pieces[:-1]:
-                store_scores("scalar", *piece)
-            for piece in pieces[-1:]:
-                vector_reads.append((step + VECTOR_READS_SCORES_AFTER, store_scores, piece))
+            for item in pieces[: len(pieces) - VECTOR_PIECES]:
+                store_scores("scalar", *item)
+            for item in pieces[len(pieces) - VECTOR_PIECES :]:
+                vector_reads.append((step + VECTOR_READS_SCORES_AFTER, store_scores, item))
             for unit in ready:
-                group_projection("scalar", unit, 0)
-                if unit == UNITS[-1]:
-                    vector_reads.append((step + VECTOR_READS_PROJECTION_AFTER, group_projection, (unit, 1)))
-                else:
-                    group_projection("scalar", unit, 1)
+                for g in range(unit[3] // GROUP):
+                    if unit == UNITS[-1] and g == unit[3] // GROUP - 1:
+                        vector_reads.append((step + VECTOR_READS_PROJECTION_AFTER, group_projection, (unit, g)))
+                    else:
+                        group_projection("scalar", unit, g)
             if step >= 1:
                 waiting = []

@@ -38,7 +38,9 @@ LAG = 3
 
 PIECE_WIDTH = (WIDTH, WIDTH // 2)
 
-VECTOR_PIECES = 1
+VECTOR_PIECES = (0, 1)
+
+VECTOR_TILES = ((6, 0), (6, 1), (7, 1))
 
 VECTOR_READS_SCORES_AFTER = 1
 VECTOR_READS_PROJECTION_AFTER = 1
@@ -288,13 +290,14 @@ def tile_sttm_single_pa_kernel(tc, left_feat, right_feat, wq, wk, out):
                 for g in range(unit[3] // GROUP):
                     project(unit, g)
 
-            for item in pieces[: len(pieces) - VECTOR_PIECES]:
-                store_scores("scalar", *item)
-            for item in pieces[len(pieces) - VECTOR_PIECES :]:
-                vector_reads.append((step + VECTOR_READS_SCORES_AFTER, store_scores, item))
+            for number, item in enumerate(pieces):
+                if number < len(pieces) - VECTOR_PIECES[item[0]]:
+                    store_scores("scalar", *item)
+                else:
+                    vector_reads.append((step + VECTOR_READS_SCORES_AFTER, store_scores, item))
             for unit in ready:
                 for g in range(unit[3] // GROUP):
-                    if unit == UNITS[-1] and g == unit[3] // GROUP - 1:
+                    if (UNITS.index(unit), g) in VECTOR_TILES:
                         vector_reads.append((step + VECTOR_READS_PROJECTION_AFTER, group_projection, (unit, g)))
                     else:
                         group_projection("scalar", unit, g)

@@ -121,21 +121,16 @@ def tile_sttm_single_pa_kernel(tc, left_feat, right_feat, wq, wk, out):
             else:
                 nc.vector.tensor_copy(out=dst, in_=src)
 
-        def transpose_weights(side, half):
-            bank = psum.tile([P, 2, 2, P], F32, tag="bank", name="w_bank_%s%d" % (side, half))
-            banks["w", side, half] = bank
+        def transpose_weights(side, slot):
+            bank = psum.tile([P, 2, P], F32, tag="bank", name="w_bank_%s%d" % (side, slot))
+            banks["w", side, slot] = bank
             words = w_raw[side][:].bitcast(F32)
-            for s in range(2):
-                for u in range(2):
-                    nc.tensor.transpose(bank[:, s, u, :], words[:, 2 * half + s, u : CHANNELS // 2 : 2], identity[:])
+            for u in range(2):
+                nc.tensor.transpose(bank[:, u, :], words[:, slot, u : CHANNELS // 2 : 2], identity[:])
 
-        def group_weights(side, half):
-            dst = w_grouped[side][:, HALF * PACK * half : HALF * PACK * (half + 1)].bitcast(F32)
-            copy(
-                "scalar",
-                dst.rearrange("p (s m u) -> p s m u", s=2, u=2),
-                banks["w", side, half][:].rearrange("p s u m -> p s m u"),
-            )
+        def group_weights(side, slot):
+            dst = w_grouped[side][:, P * PACK * slot : P * PACK * (slot + 1)].bitcast(F32)
+            copy("scalar", dst.rearrange("p (m u) -> p m u", u=2), banks["w", side, slot][:].rearrange("p u m -> p m u"))
 
         def quantize_weights(side):
             for half in range(2):
@@ -236,15 +231,14 @@ def tile_sttm_single_pa_kernel(tc, left_feat, right_feat, wq, wk, out):
         warm_bank = psum.tile([P, WIDTH], F32, tag="bank", name="warm_bank")
 
         warm_up(WARM_UP_AT_START)
-        transpose_weights(SIDES[0], 0)
-        transpose_weights(SIDES[0], 1)
+        for slot in range(PACK):
+            transpose_weights(SIDES[0], slot)
         warm_up(WARM_UP_BETWEEN_WEIGHTS)
-        group_weights(SIDES[0], 0)
-        group_weights(SIDES[0], 1)
-        transpose_weights(SIDES[1], 0)
-        transpose_weights(SIDES[1], 1)
-        group_weights(SIDES[1], 0)
-        group_weights(SIDES[1], 1)
+        for slot in range(PACK):
+            group_weights(SIDES[0], slot)
+        for slot in range(PACK):
+            transpose_weights(SIDES[1], slot)
+            group_weights(SIDES[1], slot)
 
         quantised = []
         multiplied = []

from contextlib import ExitStack

import concourse.mybir as mybir
from concourse.masks import make_identity

F32 = mybir.dt.float32
BF16 = mybir.dt.bfloat16
U32 = mybir.dt.uint32
U8 = mybir.dt.uint8
FP8X4 = mybir.dt.float8_e4m3fn_x4
STAGE1_PSUM = BF16

P = 128
PACK = 4
CHANNELS = 512
WIDTH = 512
GROUP = 128
HALF = CHANNELS // 2
PSUM_BANKS = 8
SCALE = 0.125

FLOPS = 2 * 2 * CHANNELS * CHANNELS * 2 * WIDTH + 2 * 2 * WIDTH * WIDTH * CHANNELS

SIDES = ("r", "l")

UNITS = (
    ("r", 0, 0, 256),
    ("r", 0, 256, 256),
    ("l", 0, 0, 256),
    ("l", 0, 256, 256),
    ("r", 1, 0, 256),
    ("l", 1, 0, 256),
    ("l", 1, 256, 256),
    ("r", 1, 256, 256),
)

LAG = 3

PIECE_WIDTH = (WIDTH, WIDTH // 2)

VECTOR_PIECES = (0, 1)

VECTOR_TILES = ((6, 0), (6, 1), (7, 1))

VECTOR_READS_SCORES_AFTER = 1
VECTOR_READS_PROJECTION_AFTER = 1

WARM_UP_AT_START = 4
WARM_UP_BETWEEN_WEIGHTS = 2


def tile_sttm_single_pa_kernel(tc, left_feat, right_feat, wq, wk, out):
    nc = tc.nc
    with ExitStack() as ctx:
        keep = ctx.enter_context(tc.tile_pool(name="keep", bufs=1))
        psum = ctx.enter_context(tc.psum_pool(name="psum", bufs=PSUM_BANKS))
        ctx.enter_context(tc.manual_schedule())

        features = {
            "l": left_feat[0].rearrange("(p j) h w -> p j h w", j=PACK),
            "r": right_feat[0].rearrange("(p j) h w -> p j h w", j=PACK),
        }
        weights = {
            "l": wq.rearrange("(m t) c -> m t c", t=PACK),
            "r": wk.rearrange("(m t) c -> m t c", t=PACK),
        }

        w_raw = {}
        w_grouped = {}
        w_codes = {}
        w_scales = {}
        for side in SIDES:
            w_raw[side] = keep.tile([P, PACK, CHANNELS], BF16, name="w_raw_" + side)
            w_grouped[side] = keep.tile([P, CHANNELS * PACK], BF16, name="w_grouped_" + side, align_bytes=64)
            w_codes[side] = keep.tile([P, CHANNELS], U32, name="w_codes_" + side, align_bytes=64)
            w_scales[side] = keep.tile([P, CHANNELS], U8, name="w_scales_" + side, align_bytes=64)

        x_raw = {}
        x_grouped = {}
        x_codes = {}
        x_scales = {}
        for unit in UNITS:
            tail = "_%s%d_%d_%d" % unit
            count = unit[3]
            x_raw[unit] = keep.tile([P, PACK, count], BF16, name="x_raw" + tail)
            x_grouped[unit] = keep.tile([P, count * PACK], BF16, name="x_grouped" + tail, align_bytes=64)
            x_codes[unit] = keep.tile([P, count], U32, name="x_codes" + tail, align_bytes=64)
            x_scales[unit] = keep.tile([P, count], U8, name="x_scales" + tail, align_bytes=64)

        y_grouped = {}
        y_codes = {}
        y_scales = {}
        scores_sb = {}
        for h in range(2):
            for side in SIDES:
                tail = "_%s%d" % (side, h)
                y_grouped[side, h] = keep.tile([P, WIDTH * PACK], BF16, name="y_grouped" + tail, align_bytes=64)
                y_codes[side, h] = keep.tile([P, WIDTH], U32, name="y_codes" + tail, align_bytes=64)
                y_scales[side, h] = keep.tile([P, WIDTH], U8, name="y_scales" + tail, align_bytes=64)
            for wt in range(WIDTH // P):
                for part in range(WIDTH // PIECE_WIDTH[h]):
                    scores_sb[h, wt, part] = keep.tile([P, PIECE_WIDTH[h]], F32, name="scores_sb_%d%d%d" % (h, wt, part))

        banks = {}

        def load_weights(side, half):
            slots = slice(2 * half, 2 * half + 2)
            nc.sync.dma_start(out=w_raw[side][:, slots, :], in_=weights[side][:, slots, :])

        def load_features(unit):
            side, h, first, count = unit
            nc.sync.dma_start(out=x_raw[unit][:], in_=features[side][:, :, h, first : first + count])

        def warm_up(count):
            for i in range(count):
                nc.tensor.matmul(out=warm_bank[:], lhsT=zeros[:, WIDTH:], rhs=zeros[:, :WIDTH], start=True, stop=True)

        def copy(engine, dst, src):
            if engine == "scalar":
                nc.scalar.copy(out=dst, in_=src)
            else:
                nc.vector.tensor_copy(out=dst, in_=src)

        def transpose_weights(side, slot):
            bank = psum.tile([P, 2, P], F32, tag="bank", name="w_bank_%s%d" % (side, slot))
            banks["w", side, slot] = bank
            words = w_raw[side][:].bitcast(F32)
            for u in range(2):
                nc.tensor.transpose(bank[:, u, :], words[:, slot, u : CHANNELS // 2 : 2], identity[:])

        def group_weights(side, slot):
            dst = w_grouped[side][:, P * PACK * slot : P * PACK * (slot + 1)].bitcast(F32)
            copy("scalar", dst.rearrange("p (m u) -> p m u", u=2), banks["w", side, slot][:].rearrange("p u m -> p m u"))

        def quantize_weights(side):
            for half in range(2):
                cols = slice(HALF * half, HALF * (half + 1))
                nc.vector.quantize_mx(
                    out=w_codes[side][:, cols].bitcast(FP8X4),
                    scales=w_scales[side][:, cols],
                    in_=w_grouped[side][:, HALF * PACK * half : HALF * PACK * (half + 1)],
                )

        def interleave_features(unit):
            nc.vector.tensor_copy(
                out=x_grouped[unit][:].rearrange("p (b i j) -> p b j i", i=4, j=PACK),
                in_=x_raw[unit][:].rearrange("p j (b i) -> p b j i", i=4),
            )

        def quantize_features(unit):
            nc.vector.quantize_mx(out=x_codes[unit][:].bitcast(FP8X4), scales=x_scales[unit][:], in_=x_grouped[unit][:])

        def project(unit, g):
            side = unit[0]
            bank = psum.tile([P, PACK, GROUP], STAGE1_PSUM, tag="bank", name="y_bank_%s%d_%d_%d_%d" % (unit + (g,)))
            banks["y", unit, g] = bank
            positions = slice(GROUP * g, GROUP * (g + 1))
            for t in range(PACK):
                channels = slice(P * t, P * (t + 1))
                nc.tensor.matmul_mx(
                    out=bank[:, t, :],
                    lhsT=w_codes[side][:, channels].bitcast(FP8X4),
                    lhsT_scale=w_scales[side][:, channels],
                    rhs=x_codes[unit][:, positions].bitcast(FP8X4),
                    rhs_scale=x_scales[unit][:, positions],
                    start=True,
                    stop=True,
                )

        def group_projection(engine, unit, g):
            side, h, first, count = unit
            start = (first + GROUP * g) * PACK
            copy(
                engine,
                y_grouped[side, h][:, start : start + GROUP * PACK].rearrange("p (n t) -> p n t", t=PACK),
                banks["y", unit, g][:].rearrange("p t n -> p n t"),
            )

        def quantize_projection(unit):
            side, h, first, count = unit
            positions = slice(first, first + count)
            nc.vector.quantize_mx(
                out=y_codes[side, h][:, positions].bitcast(FP8X4),
                scales=y_scales[side, h][:, positions],
                in_=y_grouped[side, h][:, first * PACK : (first + count) * PACK],
            )

        def multiply_scores(h, wt, part):
            width = PIECE_WIDTH[h]
            bank = psum.tile([P, width], F32, tag="bank", name="scores_bank_%d%d%d" % (h, wt, part))
            banks["scores", h, wt, part] = bank
            rows = slice(P * wt, P * (wt + 1))
            columns = slice(width * part, width * (part + 1))
            nc.tensor.matmul_mx(
                out=bank[:],
                lhsT=y_codes["l", h][:, rows].bitcast(FP8X4),
                lhsT_scale=y_scales["l", h][:, rows],
                rhs=y_codes["r", h][:, columns].bitcast(FP8X4),
                rhs_scale=y_scales["r", h][:, columns],
                start=True,
                stop=True,
            )

        def store_scores(engine, h, wt, part):
            width = PIECE_WIDTH[h]
            if engine == "scalar":
                nc.scalar.mul(scores_sb[h, wt, part][:], banks["scores", h, wt, part][:], SCALE)
            else:
                nc.vector.tensor_scalar_mul(scores_sb[h, wt, part][:], banks["scores", h, wt, part][:], SCALE)
            nc.sync.dma_start(
                out=out[0, h, P * wt : P * (wt + 1), width * part : width * (part + 1)], in_=scores_sb[h, wt, part][:]
            )

        load_features(UNITS[0])
        load_weights(SIDES[0], 0)
        load_weights(SIDES[0], 1)
        load_features(UNITS[1])
        load_weights(SIDES[1], 0)
        load_weights(SIDES[1], 1)
        for unit in UNITS[2:]:
            load_features(unit)

        identity = keep.tile([P, P], F32, name="identity")
        make_identity(nc, identity[:])
        table_in = keep.tile([P, 8], F32, name="table_in")
        table_out = keep.tile([P, 8], F32, name="table_out")
        nc.vector.memset(table_in[:], 0.0)
        nc.scalar.mul(table_out[:], table_in[:], SCALE)
        zeros = keep.tile([P, WIDTH + P], BF16, name="zeros")
        nc.vector.memset(zeros[:], 0.0)
        warm_bank = psum.tile([P, WIDTH], F32, tag="bank", name="warm_bank")

        warm_up(WARM_UP_AT_START)
        for slot in range(PACK):
            transpose_weights(SIDES[0], slot)
        warm_up(WARM_UP_BETWEEN_WEIGHTS)
        for slot in range(PACK):
            group_weights(SIDES[0], slot)
        for slot in range(PACK):
            transpose_weights(SIDES[1], slot)
            group_weights(SIDES[1], slot)

        quantised = []
        multiplied = []

        def covered(side, h, first, end):
            return sum(u[3] for u in quantised if u[0] == side and u[1] == h and first <= u[2] and u[2] + u[3] <= end) + sum(
                end - first for u in quantised if u[0] == side and u[1] == h and u[2] <= first and end <= u[2] + u[3] and u[3] > end - first
            ) == end - first

        vector_reads = []
        waiting = []
        for step in range(len(UNITS) + LAG + 1):
            if step < len(UNITS):
                interleave_features(UNITS[step])
            if 1 <= step <= len(SIDES):
                quantize_weights(SIDES[step - 1])
            if LAG <= step < len(UNITS) + LAG:
                quantize_projection(UNITS[step - LAG])
            if step < len(UNITS):
                quantize_features(UNITS[step])
            for due, read, args in vector_reads:
                if due == step:
                    read("vector", *args)

            pieces = []
            if LAG <= step < len(UNITS) + LAG:
                quantised.append(UNITS[step - LAG])
                for h in range(2):
                    for wt in range(WIDTH // P):
                        for part in range(WIDTH // PIECE_WIDTH[h]):
                            item = (h, wt, part)
                            q_there = covered("l", h, P * wt, P * (wt + 1))
                            k_there = covered("r", h, PIECE_WIDTH[h] * part, PIECE_WIDTH[h] * (part + 1))
                            if item not in multiplied and q_there and k_there:
                                pieces.append(item)
                                multiplied.append(item)
            for item in pieces:
                multiply_scores(*item)
            if step < len(UNITS):
                waiting.append(UNITS[step])
            ready = waiting if step >= 1 else []
            for unit in ready:
                for g in range(unit[3] // GROUP):
                    project(unit, g)

            for number, item in enumerate(pieces):
                if number < len(pieces) - VECTOR_PIECES[item[0]]:
                    store_scores("scalar", *item)
                else:
                    vector_reads.append((step + VECTOR_READS_SCORES_AFTER, store_scores, item))
            for unit in ready:
                for g in range(unit[3] // GROUP):
                    if (UNITS.index(unit), g) in VECTOR_TILES:
                        vector_reads.append((step + VECTOR_READS_PROJECTION_AFTER, group_projection, (unit, g)))
                    else:
                        group_projection("scalar", unit, g)
            if step >= 1:
                waiting = []
